import numpy as np
import ml_dtypes


def mxq(x, axis, fmt="e4m3"):
    dtype, down = {"e4m3": (ml_dtypes.float8_e4m3fn, 7), "e5m2": (ml_dtypes.float8_e5m2, 14)}[fmt]
    v = np.moveaxis(np.asarray(x, np.float32).astype(ml_dtypes.bfloat16).astype(np.float64), axis, -1)
    blocks = v.reshape(v.shape[:-1] + (-1, 32))
    amax = np.abs(blocks).max(-1, keepdims=True)
    byte = np.maximum(np.where(amax > 0, np.frexp(amax)[1] - 1 + 127, 0) - down, 1)
    scale = np.exp2(byte - 127.0)
    codes = (blocks / scale).astype(np.float32).astype(dtype).astype(np.float64)
    return np.moveaxis((codes * scale).reshape(v.shape), -1, axis)


WIDE = False


def mx_kscale(k):
    if not WIDE:
        return np.ones(k)
    levels = np.array([10, -10, 5, -5, 0])
    a = np.random.permutation(np.resize(levels, k // 512 * 4)).reshape(k // 512, 4)
    idx = np.arange(k)
    return np.exp2(a[idx // 512, idx % 128 // 32])


BF16 = ml_dtypes.bfloat16


def bf(x):
    return np.asarray(x, np.float32).astype(BF16)


def f64(x):
    return np.asarray(x).astype(np.float64)


B, C, D, T, H, W, P = 4, 1024, 512, 8, 16, 16, 2
N = T * H * W
NP = T * (H // P) * (W // P)


def setup_inputs():
    s, t = mx_kscale(D), mx_kscale(NP)
    return {"theta_x": bf(np.random.standard_normal((B, D, N)) * 2.0 * s[None, :, None]),
            "phi_x": bf((1.03 + 0.7 * np.random.standard_normal((B, D, NP))) / s[None, :, None] * t[None, None, :]),
            "g_x": bf(0.15 * (1.03 + 0.7 * np.random.standard_normal((B, D, NP))) / t[None, None, :])}


def reference(theta_x, phi_x, g_x):
    f = (mxq(f64(theta_x), 1, "e4m3").transpose(0, 2, 1) @ mxq(f64(phi_x), 1, "e4m3")) / NP
    return mxq(f64(g_x), 2, "e4m3") @ mxq(f, 2, "e4m3").transpose(0, 2, 1)

@@ -1,0 +1,202 @@
+from contextlib import ExitStack
+
+import concourse.mybir as mybir
+from concourse.masks import make_identity
+
+BF16 = mybir.dt.bfloat16
+F32 = mybir.dt.float32
+U32 = mybir.dt.uint32
+U8 = mybir.dt.uint8
+FP8X4 = mybir.dt.float8_e4m3fn_x4
+
+P = 128
+PACK = 4
+BATCH = 4
+D = 512
+N = 2048
+NP = 512
+CHUNK = 512
+SUB = 128
+CHUNKS_PER_BATCH = N // CHUNK
+STEPS = BATCH * CHUNKS_PER_BATCH
+TILES = 4
+
+FLOPS = 2 * 2 * BATCH * N * NP * D
+
+
+def tile_nonlocalblocknd_pb_t_kernel(tc, theta_x, phi_x, g_x, out):
+    nc = tc.nc
+    with ExitStack() as ctx:
+        inputs = ctx.enter_context(tc.tile_pool(name="inputs", bufs=BATCH))
+        consts = ctx.enter_context(tc.tile_pool(name="consts", bufs=1))
+        weights = ctx.enter_context(tc.tile_pool(name="weights", bufs=2))
+        stream = ctx.enter_context(tc.tile_pool(name="stream", bufs=3))
+        results = ctx.enter_context(tc.tile_pool(name="results", bufs=8))
+        psum_f = ctx.enter_context(tc.psum_pool(name="psum_f", bufs=4))
+        psum_y = ctx.enter_context(tc.psum_pool(name="psum_y", bufs=4))
+
+        theta_raw, phi_raw, g_raw = {}, {}, {}
+        phi_grouped, g_grouped = {}, {}
+        phi_mx, g_mx = {}, {}
+        theta_grouped, theta_mx = {}, {}
+        f_grouped, f_mx = {}, {}
+
+        identity = consts.tile([P, P], F32, name="identity")
+        make_identity(nc, identity[:])
+
+        def load_batch(b):
+            phi_raw[b] = inputs.tile([P, PACK, NP], BF16, name="phi_raw")
+            nc.sync.dma_start(out=phi_raw[b][:], in_=phi_x[b].rearrange("(p j) m -> p j m", j=PACK))
+            theta_raw[b] = inputs.tile([P, PACK, N], BF16, name="theta_raw")
+            g_raw[b] = inputs.tile([P, TILES * NP], BF16, name="g_raw")
+            theta_rows = theta_x[b].rearrange("(p j) n -> p j n", j=PACK)
+            pieces = CHUNKS_PER_BATCH if b == 0 else 1
+            width = N // pieces
+            for piece in range(pieces):
+                cols = slice(piece * width, (piece + 1) * width)
+                nc.sync.dma_start(out=theta_raw[b][:, :, cols], in_=theta_rows[:, :, cols])
+                if piece == 0:
+                    nc.sync.dma_start(
+                        out=g_raw[b][:], in_=g_x[b].rearrange("(i t) m -> i (t m)", t=TILES)
+                    )
+
+        def regroup_phi(b):
+            phi_grouped[b] = weights.tile(
+                [P, TILES, P, PACK], BF16, name="phi_grouped", bufs=1, align_bytes=64
+            )
+            nc.vector.tensor_copy(
+                out=phi_grouped[b][:],
+                in_=phi_raw[b][:].rearrange("p j (i t) -> p t i j", t=TILES),
+            )
+
+        def transpose_g(b):
+            g_words = g_raw[b][:].bitcast(F32).rearrange("i (t p u) -> i t u p", t=TILES, u=2)
+            g_grouped[b] = weights.tile(
+                [P, TILES * P * PACK], BF16, name="g_grouped", bufs=1, align_bytes=64
+            )
+            grouped_words = (
+                g_grouped[b][:].bitcast(F32).rearrange("p (t i u) -> p t i u", t=TILES, u=2)
+            )
+            for pair in range(TILES // 2):
+                g_ps = psum_f.tile([P, 2, 2, P], F32, name="g_ps", tag="f_ps")
+                for t in range(2):
+                    for u in range(2):
+                        nc.tensor.transpose(
+                            g_ps[:, t, u, :], g_words[:, 2 * pair + t, u, :], identity[:]
+                        )
+                nc.scalar.copy(
+                    out=grouped_words[:, 2 * pair : 2 * pair + 2, :, :],
+                    in_=g_ps[:].rearrange("p t u i -> p t i u"),
+                )
+
+        def quantise(pool, name, grouped):
+            codes = pool.tile([P, CHUNK], U32, name=name + "_codes", align_bytes=64)
+            scales = pool.tile([P, CHUNK], U8, name=name + "_scales", align_bytes=64)
+            nc.vector.quantize_mx(out=codes[:].bitcast(FP8X4), scales=scales[:], in_=grouped)
+            return codes, scales
+
+        def quantise_phi(b):
+            phi_mx[b] = quantise(weights, "phi", phi_grouped[b][:].rearrange("p t i j -> p (t i j)"))
+
+        def quantise_g(b):
+            g_mx[b] = quantise(weights, "g", g_grouped[b][:])
+
+        def regroup_theta(s):
+            b, c = divmod(s, CHUNKS_PER_BATCH)
+            theta_grouped[s] = stream.tile([P, CHUNK, PACK], BF16, name="theta_grouped", align_bytes=64)
+            nc.vector.tensor_copy(
+                out=theta_grouped[s][:].rearrange("p (c i) j -> p c j i", i=4),
+                in_=theta_raw[b][:, :, c * CHUNK : (c + 1) * CHUNK].rearrange(
+                    "p j (c i) -> p c j i", i=4
+                ),
+            )
+
+        def quantise_theta(s):
+            theta_mx[s] = quantise(stream, "theta", theta_grouped[s][:].rearrange("p n j -> p (n j)"))
+
+        def first_product(s):
+            b = s // CHUNKS_PER_BATCH
+            phi_codes, phi_scales = phi_mx[b]
+            theta_codes, theta_scales = theta_mx[s]
+            f_grouped[s] = stream.tile([P, CHUNK, PACK], BF16, name="f_grouped", align_bytes=64)
+            for sub in range(CHUNK // SUB):
+                n_cols = slice(sub * SUB, (sub + 1) * SUB)
+                f_ps = psum_f.tile([P, TILES, SUB], F32, name="f_ps")
+                for t in range(TILES):
+                    m_cols = slice(t * P, (t + 1) * P)
+                    nc.tensor.matmul_mx(
+                        out=f_ps[:, t, :],
+                        lhsT=phi_codes[:, m_cols].bitcast(FP8X4),
+                        lhsT_scale=phi_scales[:, m_cols],
+                        rhs=theta_codes[:, n_cols].bitcast(FP8X4),
+                        rhs_scale=theta_scales[:, n_cols],
+                        start=True,
+                        stop=True,
+                    )
+                nc.scalar.mul(
+                    out=f_grouped[s][:, n_cols, :],
+                    in_=f_ps[:].rearrange("p t n -> p n t"),
+                    mul=1.0 / NP,
+                )
+
+        def quantise_f(s):
+            f_mx[s] = quantise(stream, "f", f_grouped[s][:].rearrange("p n t -> p (n t)"))
+
+        def second_product(s, vector_banks):
+            b, c = divmod(s, CHUNKS_PER_BATCH)
+            g_codes, g_scales = g_mx[b]
+            f_codes, f_scales = f_mx[s]
+            y_sb = results.tile([P, TILES, CHUNK], F32, name="y_sb")
+            for t in range(TILES):
+                d_cols = slice(t * P, (t + 1) * P)
+                y_ps = psum_y.tile([P, CHUNK], F32, name="y_ps")
+                nc.tensor.matmul_mx(
+                    out=y_ps[:],
+                    lhsT=g_codes[:, d_cols].bitcast(FP8X4),
+                    lhsT_scale=g_scales[:, d_cols],
+                    rhs=f_codes[:].bitcast(FP8X4),
+                    rhs_scale=f_scales[:],
+                    start=True,
+                    stop=True,
+                )
+                if t < TILES - vector_banks:
+                    nc.scalar.copy(out=y_sb[:, t, :], in_=y_ps[:])
+                else:
+                    nc.vector.tensor_copy(out=y_sb[:, t, :], in_=y_ps[:])
+            nc.sync.dma_start(
+                out=out[b].rearrange("(i t) n -> i t n", t=TILES)[:, :, c * CHUNK : (c + 1) * CHUNK],
+                in_=y_sb[:],
+            )
+
+        for b in range(BATCH):
+            load_batch(b)
+
+        regroup_phi(0)
+        regroup_theta(0)
+        quantise_phi(0)
+        quantise_theta(0)
+        transpose_g(0)
+        first_product(0)
+        regroup_theta(1)
+        quantise_g(0)
+        quantise_theta(1)
+        regroup_theta(2)
+
+        for s in range(STEPS):
+            b, c = divmod(s, CHUNKS_PER_BATCH)
+            prepare = b + 1 < BATCH
+            quantise_f(s)
+            if s + 1 < STEPS:
+                first_product(s + 1)
+            if s + 3 < STEPS:
+                regroup_theta(s + 3)
+            if s + 2 < STEPS:
+                quantise_theta(s + 2)
+            if prepare and c == 1:
+                regroup_phi(b + 1)
+            if prepare and c == 2:
+                quantise_phi(b + 1)
+                quantise_g(b + 1)
+            second_product(s, vector_banks=1 if prepare and c in (1, 2) else 2)
+            if prepare and c == 1:
+                transpose_g(b + 1)

@@ -35,6 +35,8 @@ def tile_nonlocalblocknd_pb_t_kernel(tc, theta_x, phi_x, g_x, out):
         psum_f = ctx.enter_context(tc.psum_pool(name="psum_f", bufs=4))
         psum_y = ctx.enter_context(tc.psum_pool(name="psum_y", bufs=4))
 
+        ctx.enter_context(tc.manual_schedule())
+
         theta_raw, phi_raw, g_raw = {}, {}, {}
         phi_grouped, g_grouped = {}, {}
         phi_mx, g_mx = {}, {}

@@ -31,7 +31,7 @@ def tile_nonlocalblocknd_pb_t_kernel(tc, theta_x, phi_x, g_x, out):
         consts = ctx.enter_context(tc.tile_pool(name="consts", bufs=1))
         weights = ctx.enter_context(tc.tile_pool(name="weights", bufs=2))
         stream = ctx.enter_context(tc.tile_pool(name="stream", bufs=3))
-        results = ctx.enter_context(tc.tile_pool(name="results", bufs=8))
+        results = ctx.enter_context(tc.tile_pool(name="results", bufs=8 * TILES))
         psum_f = ctx.enter_context(tc.psum_pool(name="psum_f", bufs=4))
         psum_y = ctx.enter_context(tc.psum_pool(name="psum_y", bufs=4))
 
@@ -144,11 +144,11 @@ def tile_nonlocalblocknd_pb_t_kernel(tc, theta_x, phi_x, g_x, out):
         def quantise_f(s):
             f_mx[s] = quantise(stream, "f", f_grouped[s][:].rearrange("p n t -> p (n t)"))
 
-        def second_product(s, vector_banks):
+        def second_product(s, vector_tiles):
             b, c = divmod(s, CHUNKS_PER_BATCH)
             g_codes, g_scales = g_mx[b]
             f_codes, f_scales = f_mx[s]
-            y_sb = results.tile([P, TILES, CHUNK], F32, name="y_sb")
+            out_rows = out[b].rearrange("(i t) n -> i t n", t=TILES)
             for t in range(TILES):
                 d_cols = slice(t * P, (t + 1) * P)
                 y_ps = psum_y.tile([P, CHUNK], F32, name="y_ps")
@@ -161,14 +161,12 @@ def tile_nonlocalblocknd_pb_t_kernel(tc, theta_x, phi_x, g_x, out):
                     start=True,
                     stop=True,
                 )
-                if t < TILES - vector_banks:
-                    nc.scalar.copy(out=y_sb[:, t, :], in_=y_ps[:])
+                y_sb = results.tile([P, CHUNK], F32, name="y_sb")
+                if t in vector_tiles:
+                    nc.vector.tensor_copy(out=y_sb[:], in_=y_ps[:])
                 else:
-                    nc.vector.tensor_copy(out=y_sb[:, t, :], in_=y_ps[:])
-            nc.sync.dma_start(
-                out=out[b].rearrange("(i t) n -> i t n", t=TILES)[:, :, c * CHUNK : (c + 1) * CHUNK],
-                in_=y_sb[:],
-            )
+                    nc.scalar.copy(out=y_sb[:], in_=y_ps[:])
+                nc.sync.dma_start(out=out_rows[:, t, c * CHUNK : (c + 1) * CHUNK], in_=y_sb[:])
 
         for b in range(BATCH):
             load_batch(b)
@@ -199,6 +197,6 @@ def tile_nonlocalblocknd_pb_t_kernel(tc, theta_x, phi_x, g_x, out):
             if prepare and c == 2:
                 quantise_phi(b + 1)
                 quantise_g(b + 1)
-            second_product(s, vector_banks=1 if prepare and c in (1, 2) else 2)
+            second_product(s, vector_tiles=(3,) if prepare and c in (1, 2) else (1, 3))
             if prepare and c == 1:
                 transpose_g(b + 1)

@@ -49,14 +49,16 @@ def tile_nonlocalblocknd_pb_t_kernel(tc, theta_x, phi_x, g_x, out):
         def load_batch(b):
             phi_raw[b] = inputs.tile([P, PACK, NP], BF16, name="phi_raw")
             nc.sync.dma_start(out=phi_raw[b][:], in_=phi_x[b].rearrange("(p j) m -> p j m", j=PACK))
-            theta_raw[b] = inputs.tile([P, PACK, N], BF16, name="theta_raw")
             g_raw[b] = inputs.tile([P, TILES * NP], BF16, name="g_raw")
             theta_rows = theta_x[b].rearrange("(p j) n -> p j n", j=PACK)
             pieces = CHUNKS_PER_BATCH if b == 0 else 1
             width = N // pieces
             for piece in range(pieces):
                 cols = slice(piece * width, (piece + 1) * width)
-                nc.sync.dma_start(out=theta_raw[b][:, :, cols], in_=theta_rows[:, :, cols])
+                raw = inputs.tile([P, PACK, width], BF16, name="theta_raw", tag="theta_raw%d" % width, bufs=4 if b == 0 else 3)
+                nc.sync.dma_start(out=raw[:], in_=theta_rows[:, :, cols])
+                for k in range(width // CHUNK):
+                    theta_raw[(b * N + piece * width) // CHUNK + k] = raw[:, :, k * CHUNK : (k + 1) * CHUNK]
                 if piece == 0:
                     nc.sync.dma_start(
                         out=g_raw[b][:], in_=g_x[b].rearrange("(i t) m -> i (t m)", t=TILES)
@@ -104,13 +106,10 @@ def tile_nonlocalblocknd_pb_t_kernel(tc, theta_x, phi_x, g_x, out):
             g_mx[b] = quantise(weights, "g", g_grouped[b][:])
 
         def regroup_theta(s):
-            b, c = divmod(s, CHUNKS_PER_BATCH)
             theta_grouped[s] = stream.tile([P, CHUNK, PACK], BF16, name="theta_grouped", align_bytes=64)
             nc.vector.tensor_copy(
                 out=theta_grouped[s][:].rearrange("p (c i) j -> p c j i", i=4),
-                in_=theta_raw[b][:, :, c * CHUNK : (c + 1) * CHUNK].rearrange(
-                    "p j (c i) -> p c j i", i=4
-                ),
+                in_=theta_raw[s].rearrange("p j (c i) -> p c j i", i=4),
             )
 
         def quantise_theta(s):

@@ -46,34 +46,39 @@ def tile_nonlocalblocknd_pb_t_kernel(tc, theta_x, phi_x, g_x, out):
         identity = consts.tile([P, P], F32, name="identity")
         make_identity(nc, identity[:])
 
-        def load_batch(b):
+        def load_phi(b):
             phi_raw[b] = inputs.tile([P, PACK, NP], BF16, name="phi_raw")
             nc.sync.dma_start(out=phi_raw[b][:], in_=phi_x[b].rearrange("(p j) m -> p j m", j=PACK))
-            g_raw[b] = inputs.tile([P, TILES * NP], BF16, name="g_raw")
-            theta_rows = theta_x[b].rearrange("(p j) n -> p j n", j=PACK)
-            pieces = CHUNKS_PER_BATCH if b == 0 else 1
-            width = N // pieces
-            for piece in range(pieces):
-                cols = slice(piece * width, (piece + 1) * width)
-                raw = inputs.tile([P, PACK, width], BF16, name="theta_raw", tag="theta_raw%d" % width, bufs=4 if b == 0 else 3)
-                nc.sync.dma_start(out=raw[:], in_=theta_rows[:, :, cols])
-                for k in range(width // CHUNK):
-                    theta_raw[(b * N + piece * width) // CHUNK + k] = raw[:, :, k * CHUNK : (k + 1) * CHUNK]
-                if piece == 0:
-                    nc.sync.dma_start(
-                        out=g_raw[b][:], in_=g_x[b].rearrange("(i t) m -> i (t m)", t=TILES)
-                    )
 
-        def regroup_phi(b):
+        def load_g(b):
+            g_raw[b] = inputs.tile([P, TILES * NP], BF16, name="g_raw")
+            nc.sync.dma_start(out=g_raw[b][:], in_=g_x[b].rearrange("(i t) m -> i (t m)", t=TILES))
+
+        def load_theta(b, chunk, chunks):
+            rows = theta_x[b].rearrange("(p j) n -> p j n", j=PACK)
+            raw = inputs.tile([P, PACK, chunks * CHUNK], BF16, name="theta_raw", tag="theta_raw%d" % chunks, bufs={1: 2, 2: 1, 4: 3}[chunks])
+            nc.sync.dma_start(out=raw[:], in_=rows[:, :, chunk * CHUNK : (chunk + chunks) * CHUNK])
+            for k in range(chunks):
+                theta_raw[b * CHUNKS_PER_BATCH + chunk + k] = raw[:, :, k * CHUNK : (k + 1) * CHUNK]
+
+        def new_phi(b):
             phi_grouped[b] = weights.tile(
                 [P, TILES, P, PACK], BF16, name="phi_grouped", bufs=1, align_bytes=64
             )
-            nc.vector.tensor_copy(
-                out=phi_grouped[b][:],
-                in_=phi_raw[b][:].rearrange("p j (i t) -> p t i j", t=TILES),
+            codes = weights.tile([P, NP], U32, name="phi_codes", align_bytes=64)
+            scales = weights.tile([P, NP], U8, name="phi_scales", align_bytes=64)
+            phi_mx[b] = codes, scales
+
+        def regroup_phi(copy, b, t0, t1):
+            copy(
+                out=phi_grouped[b][:, t0:t1].rearrange("p t i j -> p i j t"),
+                in_=phi_raw[b][:].rearrange("p j (i t) -> p i j t", t=TILES)[:, :, :, t0:t1],
             )
 
-        def transpose_g(b):
+        def quantise_phi(b, t0, t1):
+            quantise(phi_mx[b], phi_grouped[b][:].rearrange("p t i j -> p (t i j)"), t0 * P, t1 * P)
+
+        def transpose_g(b, copies):
             g_words = g_raw[b][:].bitcast(F32).rearrange("i (t p u) -> i t u p", t=TILES, u=2)
             g_grouped[b] = weights.tile(
                 [P, TILES * P * PACK], BF16, name="g_grouped", bufs=1, align_bytes=64
@@ -88,114 +93,156 @@ def tile_nonlocalblocknd_pb_t_kernel(tc, theta_x, phi_x, g_x, out):
                         nc.tensor.transpose(
                             g_ps[:, t, u, :], g_words[:, 2 * pair + t, u, :], identity[:]
                         )
-                nc.scalar.copy(
+                copies[pair](
                     out=grouped_words[:, 2 * pair : 2 * pair + 2, :, :],
                     in_=g_ps[:].rearrange("p t u i -> p t i u"),
                 )
 
-        def quantise(pool, name, grouped):
-            codes = pool.tile([P, CHUNK], U32, name=name + "_codes", align_bytes=64)
-            scales = pool.tile([P, CHUNK], U8, name=name + "_scales", align_bytes=64)
-            nc.vector.quantize_mx(out=codes[:].bitcast(FP8X4), scales=scales[:], in_=grouped)
-            return codes, scales
-
-        def quantise_phi(b):
-            phi_mx[b] = quantise(weights, "phi", phi_grouped[b][:].rearrange("p t i j -> p (t i j)"))
-
-        def quantise_g(b):
-            g_mx[b] = quantise(weights, "g", g_grouped[b][:])
-
-        def regroup_theta(s):
-            theta_grouped[s] = stream.tile([P, CHUNK, PACK], BF16, name="theta_grouped", align_bytes=64)
-            nc.vector.tensor_copy(
-                out=theta_grouped[s][:].rearrange("p (c i) j -> p c j i", i=4),
-                in_=theta_raw[s].rearrange("p j (c i) -> p c j i", i=4),
+        def quantise(operand, grouped, c0, c1):
+            codes, scales = operand
+            nc.vector.quantize_mx(
+                out=codes[:, c0:c1].bitcast(FP8X4), scales=scales[:, c0:c1], in_=grouped[:, c0 * PACK : c1 * PACK]
             )
 
-        def quantise_theta(s):
-            theta_mx[s] = quantise(stream, "theta", theta_grouped[s][:].rearrange("p n j -> p (n j)"))
+        def quantise_g(b):
+            codes = weights.tile([P, D], U32, name="g_codes", align_bytes=64)
+            scales = weights.tile([P, D], U8, name="g_scales", align_bytes=64)
+            g_mx[b] = codes, scales
+            quantise(g_mx[b], g_grouped[b][:], 0, D)
 
-        def first_product(s):
+        def new_theta(s):
+            theta_grouped[s] = stream.tile([P, CHUNK, PACK], BF16, name="theta_grouped", align_bytes=64)
+            codes = stream.tile([P, CHUNK], U32, name="theta_codes", align_bytes=64)
+            scales = stream.tile([P, CHUNK], U8, name="theta_scales", align_bytes=64)
+            theta_mx[s] = codes, scales
+
+        def regroup_theta(copy, s, n0, n1):
+            copy(
+                out=theta_grouped[s][:, n0:n1, :].rearrange("p (c i) j -> p c j i", i=4),
+                in_=theta_raw[s][:, :, n0:n1].rearrange("p j (c i) -> p c j i", i=4),
+            )
+
+        def quantise_theta(s, n0, n1):
+            quantise(theta_mx[s], theta_grouped[s][:].rearrange("p n j -> p (n j)"), n0, n1)
+
+        def new_f(s):
+            f_grouped[s] = stream.tile([P, CHUNK, PACK], BF16, name="f_grouped", align_bytes=64)
+
+        def first_product(s, sub):
             b = s // CHUNKS_PER_BATCH
             phi_codes, phi_scales = phi_mx[b]
             theta_codes, theta_scales = theta_mx[s]
-            f_grouped[s] = stream.tile([P, CHUNK, PACK], BF16, name="f_grouped", align_bytes=64)
-            for sub in range(CHUNK // SUB):
-                n_cols = slice(sub * SUB, (sub + 1) * SUB)
-                f_ps = psum_f.tile([P, TILES, SUB], F32, name="f_ps")
-                for t in range(TILES):
-                    m_cols = slice(t * P, (t + 1) * P)
-                    nc.tensor.matmul_mx(
-                        out=f_ps[:, t, :],
-                        lhsT=phi_codes[:, m_cols].bitcast(FP8X4),
-                        lhsT_scale=phi_scales[:, m_cols],
-                        rhs=theta_codes[:, n_cols].bitcast(FP8X4),
-                        rhs_scale=theta_scales[:, n_cols],
-                        start=True,
-                        stop=True,
-                    )
-                nc.scalar.mul(
-                    out=f_grouped[s][:, n_cols, :],
-                    in_=f_ps[:].rearrange("p t n -> p n t"),
-                    mul=1.0 / NP,
+            n_cols = slice(sub * SUB, (sub + 1) * SUB)
+            f_ps = psum_f.tile([P, TILES, SUB], F32, name="f_ps")
+            for t in range(TILES):
+                m_cols = slice(t * P, (t + 1) * P)
+                nc.tensor.matmul_mx(
+                    out=f_ps[:, t, :],
+                    lhsT=phi_codes[:, m_cols].bitcast(FP8X4),
+                    lhsT_scale=phi_scales[:, m_cols],
+                    rhs=theta_codes[:, n_cols].bitcast(FP8X4),
+                    rhs_scale=theta_scales[:, n_cols],
+                    start=True,
+                    stop=True,
                 )
+            nc.scalar.mul(
+                out=f_grouped[s][:, n_cols, :],
+                in_=f_ps[:].rearrange("p t n -> p n t"),
+                mul=1.0 / NP,
+            )
 
         def quantise_f(s):
-            f_mx[s] = quantise(stream, "f", f_grouped[s][:].rearrange("p n t -> p (n t)"))
+            codes = stream.tile([P, CHUNK], U32, name="f_codes", align_bytes=64)
+            scales = stream.tile([P, CHUNK], U8, name="f_scales", align_bytes=64)
+            f_mx[s] = codes, scales
+            quantise(f_mx[s], f_grouped[s][:].rearrange("p n t -> p (n t)"), 0, CHUNK)
 
-        def second_product(s, vector_tiles):
+        def second_product(copy, s, t):
             b, c = divmod(s, CHUNKS_PER_BATCH)
             g_codes, g_scales = g_mx[b]
             f_codes, f_scales = f_mx[s]
             out_rows = out[b].rearrange("(i t) n -> i t n", t=TILES)
-            for t in range(TILES):
-                d_cols = slice(t * P, (t + 1) * P)
-                y_ps = psum_y.tile([P, CHUNK], F32, name="y_ps")
-                nc.tensor.matmul_mx(
-                    out=y_ps[:],
-                    lhsT=g_codes[:, d_cols].bitcast(FP8X4),
-                    lhsT_scale=g_scales[:, d_cols],
-                    rhs=f_codes[:].bitcast(FP8X4),
-                    rhs_scale=f_scales[:],
-                    start=True,
-                    stop=True,
-                )
-                y_sb = results.tile([P, CHUNK], F32, name="y_sb")
-                if t in vector_tiles:
-                    nc.vector.tensor_copy(out=y_sb[:], in_=y_ps[:])
-                else:
-                    nc.scalar.copy(out=y_sb[:], in_=y_ps[:])
-                nc.sync.dma_start(out=out_rows[:, t, c * CHUNK : (c + 1) * CHUNK], in_=y_sb[:])
+            d_cols = slice(t * P, (t + 1) * P)
+            y_ps = psum_y.tile([P, CHUNK], F32, name="y_ps")
+            nc.tensor.matmul_mx(
+                out=y_ps[:],
+                lhsT=g_codes[:, d_cols].bitcast(FP8X4),
+                lhsT_scale=g_scales[:, d_cols],
+                rhs=f_codes[:].bitcast(FP8X4),
+                rhs_scale=f_scales[:],
+                start=True,
+                stop=True,
+            )
+            y_sb = results.tile([P, CHUNK], F32, name="y_sb")
+            copy(out=y_sb[:], in_=y_ps[:])
+            nc.sync.dma_start(out=out_rows[:, t, c * CHUNK : (c + 1) * CHUNK], in_=y_sb[:])
 
-        for b in range(BATCH):
-            load_batch(b)
+        vector, scalar = nc.vector.tensor_copy, nc.scalar.copy
+        HALF = CHUNK // 2
 
-        regroup_phi(0)
-        regroup_theta(0)
-        quantise_phi(0)
-        quantise_theta(0)
-        transpose_g(0)
-        first_product(0)
-        regroup_theta(1)
+        load_phi(0)
+        load_theta(0, 0, 1)
+        load_theta(0, 1, 1)
+        load_g(0)
+        load_theta(0, 2, 2)
+        for b in range(1, BATCH):
+            load_phi(b)
+            load_theta(b, 0, 4)
+            load_g(b)
+
+        new_phi(0)
+        new_theta(0)
+        regroup_phi(vector, 0, 0, 2)
+        regroup_phi(scalar, 0, 2, 4)
+        quantise_phi(0, 0, 2)
+        regroup_theta(vector, 0, 0, HALF)
+        regroup_theta(scalar, 0, HALF, CHUNK)
+        quantise_phi(0, 2, 4)
+        quantise_theta(0, 0, HALF)
+        quantise_theta(0, HALF, CHUNK)
+        new_f(0)
+        for sub in range(CHUNK // SUB):
+            first_product(0, sub)
+        new_theta(1)
+        regroup_theta(vector, 1, 0, CHUNK)
+        transpose_g(0, (scalar, scalar))
+        quantise_theta(1, 0, CHUNK)
+        new_f(1)
+        for sub in range(CHUNK // SUB):
+            first_product(1, sub)
+        new_theta(2)
+        regroup_theta(vector, 2, 0, CHUNK)
+        quantise_f(0)
+        quantise_theta(2, 0, CHUNK)
         quantise_g(0)
-        quantise_theta(1)
-        regroup_theta(2)
+        new_theta(3)
+        regroup_theta(vector, 3, 0, CHUNK)
 
         for s in range(STEPS):
             b, c = divmod(s, CHUNKS_PER_BATCH)
             prepare = b + 1 < BATCH
-            quantise_f(s)
-            if s + 1 < STEPS:
-                first_product(s + 1)
             if s + 3 < STEPS:
-                regroup_theta(s + 3)
-            if s + 2 < STEPS:
-                quantise_theta(s + 2)
+                quantise_theta(s + 3, 0, CHUNK)
             if prepare and c == 1:
-                regroup_phi(b + 1)
+                quantise_phi(b + 1, 0, TILES)
             if prepare and c == 2:
-                quantise_phi(b + 1)
                 quantise_g(b + 1)
-            second_product(s, vector_tiles=(3,) if prepare and c in (1, 2) else (1, 3))
+            if s + 2 < STEPS:
+                new_f(s + 2)
+            vector_tiles = (3,) if prepare and c < 3 else (1, 2, 3) if s in (12, 13) else (1, 3)
+            for kind, t in (("f", 0), ("y", 0), ("f", 1), ("y", 1), ("f", 2), ("y", 2), ("f", 3), ("y", 3)):
+                if kind == "y":
+                    second_product(vector if t in vector_tiles else scalar, s, t)
+                elif s + 2 < STEPS:
+                    first_product(s + 2, t)
+                if kind == "f" and t == 1:
+                    if s + 1 < STEPS:
+                        quantise_f(s + 1)
+                    if s + 4 < STEPS:
+                        new_theta(s + 4)
+                        regroup_theta(vector, s + 4, 0, CHUNK)
+            if prepare and c == 0:
+                new_phi(b + 1)
+                regroup_phi(vector, b + 1, 0, TILES)
             if prepare and c == 1:
-                transpose_g(b + 1)
+                transpose_g(b + 1, (vector, scalar))

@@ -118,8 +118,8 @@ def tile_nonlocalblocknd_pb_t_kernel(tc, theta_x, phi_x, g_x, out):
 
         def regroup_theta(copy, s, n0, n1):
             copy(
-                out=theta_grouped[s][:, n0:n1, :].rearrange("p (c i) j -> p c j i", i=4),
-                in_=theta_raw[s][:, :, n0:n1].rearrange("p j (c i) -> p c j i", i=4),
+                out=theta_grouped[s][:, n0:n1, :].rearrange("p (c i) j -> p c j i", i=8),
+                in_=theta_raw[s][:, :, n0:n1].rearrange("p j (c i) -> p c j i", i=8),
             )
 
         def quantise_theta(s, n0, n1):

@@ -56,7 +56,7 @@ def tile_nonlocalblocknd_pb_t_kernel(tc, theta_x, phi_x, g_x, out):
 
         def load_theta(b, chunk, chunks):
             rows = theta_x[b].rearrange("(p j) n -> p j n", j=PACK)
-            raw = inputs.tile([P, PACK, chunks * CHUNK], BF16, name="theta_raw", tag="theta_raw%d" % chunks, bufs={1: 2, 2: 1, 4: 3}[chunks])
+            raw = inputs.tile([P, PACK, chunks * CHUNK], BF16, name="theta_raw", tag="theta_raw%d" % chunks, bufs={1: 4, 4: 3}[chunks])
             nc.sync.dma_start(out=raw[:], in_=rows[:, :, chunk * CHUNK : (chunk + chunks) * CHUNK])
             for k in range(chunks):
                 theta_raw[b * CHUNKS_PER_BATCH + chunk + k] = raw[:, :, k * CHUNK : (k + 1) * CHUNK]
@@ -128,7 +128,7 @@ def tile_nonlocalblocknd_pb_t_kernel(tc, theta_x, phi_x, g_x, out):
         def new_f(s):
             f_grouped[s] = stream.tile([P, CHUNK, PACK], BF16, name="f_grouped", align_bytes=64)
 
-        def first_product(s, sub):
+        def first_product(s, sub, on_vector=False):
             b = s // CHUNKS_PER_BATCH
             phi_codes, phi_scales = phi_mx[b]
             theta_codes, theta_scales = theta_mx[s]
@@ -145,11 +145,13 @@ def tile_nonlocalblocknd_pb_t_kernel(tc, theta_x, phi_x, g_x, out):
                     start=True,
                     stop=True,
                 )
-            nc.scalar.mul(
-                out=f_grouped[s][:, n_cols, :],
-                in_=f_ps[:].rearrange("p t n -> p n t"),
-                mul=1.0 / NP,
-            )
+            grouped, banked = f_grouped[s][:, n_cols, :], f_ps[:].rearrange("p t n -> p n t")
+            if on_vector:
+                nc.vector.tensor_scalar(
+                    out=grouped, in0=banked, scalar1=1.0 / NP, scalar2=None, op0=mybir.AluOpType.mult
+                )
+            else:
+                nc.scalar.mul(out=grouped, in_=banked, mul=1.0 / NP)
 
         def quantise_f(s):
             codes = stream.tile([P, CHUNK], U32, name="f_codes", align_bytes=64)
@@ -184,7 +186,8 @@ def tile_nonlocalblocknd_pb_t_kernel(tc, theta_x, phi_x, g_x, out):
         load_theta(0, 0, 1)
         load_theta(0, 1, 1)
         load_g(0)
-        load_theta(0, 2, 2)
+        load_theta(0, 2, 1)
+        load_theta(0, 3, 1)
         for b in range(1, BATCH):
             load_phi(b)
             load_theta(b, 0, 4)
@@ -207,42 +210,37 @@ def tile_nonlocalblocknd_pb_t_kernel(tc, theta_x, phi_x, g_x, out):
         regroup_theta(vector, 1, 0, CHUNK)
         transpose_g(0, (scalar, scalar))
         quantise_theta(1, 0, CHUNK)
-        new_f(1)
-        for sub in range(CHUNK // SUB):
-            first_product(1, sub)
         new_theta(2)
         regroup_theta(vector, 2, 0, CHUNK)
         quantise_f(0)
-        quantise_theta(2, 0, CHUNK)
         quantise_g(0)
-        new_theta(3)
-        regroup_theta(vector, 3, 0, CHUNK)
 
         for s in range(STEPS):
             b, c = divmod(s, CHUNKS_PER_BATCH)
             prepare = b + 1 < BATCH
-            if s + 3 < STEPS:
-                quantise_theta(s + 3, 0, CHUNK)
+            y_vector = (0,) if prepare and c < 3 else (0, 1)
+            f_vector = (1, 3) if s + 2 == STEPS else ()
+            if s + 1 < STEPS:
+                new_f(s + 1)
+                for t in range(TILES):
+                    first_product(s + 1, t, t in f_vector)
+            if s + 2 < STEPS:
+                quantise_theta(s + 2, 0, CHUNK)
             if prepare and c == 1:
                 quantise_phi(b + 1, 0, TILES)
-            if prepare and c == 2:
+            if prepare and c == 3:
                 quantise_g(b + 1)
-            if s + 2 < STEPS:
-                new_f(s + 2)
-            vector_tiles = (3,) if prepare and c < 3 else (1, 2, 3) if s in (12, 13) else (1, 3)
-            for kind, t in (("f", 0), ("y", 0), ("f", 1), ("y", 1), ("f", 2), ("y", 2), ("f", 3), ("y", 3)):
-                if kind == "y":
-                    second_product(vector if t in vector_tiles else scalar, s, t)
-                elif s + 2 < STEPS:
-                    first_product(s + 2, t)
-                if kind == "f" and t == 1:
-                    if s + 1 < STEPS:
-                        quantise_f(s + 1)
-                    if s + 4 < STEPS:
-                        new_theta(s + 4)
-                        regroup_theta(vector, s + 4, 0, CHUNK)
+            if s + 3 < STEPS:
+                new_theta(s + 3)
+                regroup_theta(vector, s + 3, 0, CHUNK)
+            for t in range(TILES):
+                if t == 2:
+                    pass
+                second_product(vector if t in y_vector else scalar, s, t)
+            if s + 1 < STEPS:
+                quantise_f(s + 1)
             if prepare and c == 0:
                 new_phi(b + 1)
                 regroup_phi(vector, b + 1, 0, TILES)
-            if prepare and c == 1:
+            if prepare and c == 2:
                 transpose_g(b + 1, (vector, scalar))

@@ -69,6 +69,12 @@ def tile_nonlocalblocknd_pb_t_kernel(tc, theta_x, phi_x, g_x, out):
             scales = weights.tile([P, NP], U8, name="phi_scales", align_bytes=64)
             phi_mx[b] = codes, scales
 
+        def regroup_phi_rows(copy, b, i0, i1):
+            copy(
+                out=phi_grouped[b][:, :, i0:i1].rearrange("p t i j -> p i j t"),
+                in_=phi_raw[b][:, :, TILES * i0 : TILES * i1].rearrange("p j (i t) -> p i j t", t=TILES),
+            )
+
         def regroup_phi(copy, b, t0, t1):
             copy(
                 out=phi_grouped[b][:, t0:t1].rearrange("p t i j -> p i j t"),
@@ -218,7 +224,7 @@ def tile_nonlocalblocknd_pb_t_kernel(tc, theta_x, phi_x, g_x, out):
         for s in range(STEPS):
             b, c = divmod(s, CHUNKS_PER_BATCH)
             prepare = b + 1 < BATCH
-            y_vector = (0,) if prepare and c < 3 else (0, 1)
+            y_vector = (2, 3) if s + 2 == STEPS else (0, 1) if c == 3 or not prepare else (0,)
             f_vector = (1, 3) if s + 2 == STEPS else ()
             if s + 1 < STEPS:
                 new_f(s + 1)
@@ -226,21 +232,23 @@ def tile_nonlocalblocknd_pb_t_kernel(tc, theta_x, phi_x, g_x, out):
                     first_product(s + 1, t, t in f_vector)
             if s + 2 < STEPS:
                 quantise_theta(s + 2, 0, CHUNK)
-            if prepare and c == 1:
+            if prepare and c == 2:
                 quantise_phi(b + 1, 0, TILES)
             if prepare and c == 3:
                 quantise_g(b + 1)
             if s + 3 < STEPS:
                 new_theta(s + 3)
                 regroup_theta(vector, s + 3, 0, CHUNK)
+            if s + 1 < STEPS and s + 2 == STEPS:
+                quantise_f(s + 1)
             for t in range(TILES):
-                if t == 2:
-                    pass
                 second_product(vector if t in y_vector else scalar, s, t)
-            if s + 1 < STEPS:
+            if s + 1 < STEPS and not (s + 2 == STEPS):
                 quantise_f(s + 1)
             if prepare and c == 0:
                 new_phi(b + 1)
-                regroup_phi(vector, b + 1, 0, TILES)
+                regroup_phi_rows(vector, b + 1, 0, P // 2)
+            if prepare and c == 1:
+                regroup_phi_rows(vector, b + 1, P // 2, P)
             if prepare and c == 2:
                 transpose_g(b + 1, (vector, scalar))

@@ -56,7 +56,7 @@ def tile_nonlocalblocknd_pb_t_kernel(tc, theta_x, phi_x, g_x, out):
 
         def load_theta(b, chunk, chunks):
             rows = theta_x[b].rearrange("(p j) n -> p j n", j=PACK)
-            raw = inputs.tile([P, PACK, chunks * CHUNK], BF16, name="theta_raw", tag="theta_raw%d" % chunks, bufs={1: 4, 4: 3}[chunks])
+            raw = inputs.tile([P, PACK, chunks * CHUNK], BF16, name="theta_raw", tag="theta_raw%d" % chunks, bufs={1: 4, 2: 2, 4: 2}[chunks])
             nc.sync.dma_start(out=raw[:], in_=rows[:, :, chunk * CHUNK : (chunk + chunks) * CHUNK])
             for k in range(chunks):
                 theta_raw[b * CHUNKS_PER_BATCH + chunk + k] = raw[:, :, k * CHUNK : (k + 1) * CHUNK]
@@ -194,7 +194,11 @@ def tile_nonlocalblocknd_pb_t_kernel(tc, theta_x, phi_x, g_x, out):
         load_g(0)
         load_theta(0, 2, 1)
         load_theta(0, 3, 1)
-        for b in range(1, BATCH):
+        load_theta(1, 0, 2)
+        load_phi(1)
+        load_theta(1, 2, 2)
+        load_g(1)
+        for b in range(2, BATCH):
             load_phi(b)
             load_theta(b, 0, 4)
             load_g(b)
@@ -224,7 +228,7 @@ def tile_nonlocalblocknd_pb_t_kernel(tc, theta_x, phi_x, g_x, out):
         for s in range(STEPS):
             b, c = divmod(s, CHUNKS_PER_BATCH)
             prepare = b + 1 < BATCH
-            y_vector = (2, 3) if s + 2 == STEPS else (0, 1) if c == 3 or not prepare else (0,)
+            y_vector = (2, 3) if s + 2 == STEPS else (0, 2) if c == 3 or not prepare else (0,)
             f_vector = (1, 3) if s + 2 == STEPS else ()
             if s + 1 < STEPS:
                 new_f(s + 1)

@@ -37,6 +37,7 @@ def tile_nonlocalblocknd_pb_t_kernel(tc, theta_x, phi_x, g_x, out):
 
         ctx.enter_context(tc.manual_schedule())
 
+        HALF = CHUNK // 2
         theta_raw, phi_raw, g_raw = {}, {}, {}
         phi_grouped, g_grouped = {}, {}
         phi_mx, g_mx = {}, {}
@@ -159,11 +160,12 @@ def tile_nonlocalblocknd_pb_t_kernel(tc, theta_x, phi_x, g_x, out):
             else:
                 nc.scalar.mul(out=grouped, in_=banked, mul=1.0 / NP)
 
-        def quantise_f(s):
-            codes = stream.tile([P, CHUNK], U32, name="f_codes", align_bytes=64)
-            scales = stream.tile([P, CHUNK], U8, name="f_scales", align_bytes=64)
-            f_mx[s] = codes, scales
-            quantise(f_mx[s], f_grouped[s][:].rearrange("p n t -> p (n t)"), 0, CHUNK)
+        def quantise_f(s, n0, n1):
+            if n0 == 0:
+                codes = stream.tile([P, CHUNK], U32, name="f_codes", align_bytes=64)
+                scales = stream.tile([P, CHUNK], U8, name="f_scales", align_bytes=64)
+                f_mx[s] = codes, scales
+            quantise(f_mx[s], f_grouped[s][:].rearrange("p n t -> p (n t)"), n0, n1)
 
         def second_product(copy, s, t):
             b, c = divmod(s, CHUNKS_PER_BATCH)
@@ -185,8 +187,31 @@ def tile_nonlocalblocknd_pb_t_kernel(tc, theta_x, phi_x, g_x, out):
             copy(out=y_sb[:], in_=y_ps[:])
             nc.sync.dma_start(out=out_rows[:, t, c * CHUNK : (c + 1) * CHUNK], in_=y_sb[:])
 
+        def last_product(copy, half, pair):
+            s = STEPS - 1
+            b, c = divmod(s, CHUNKS_PER_BATCH)
+            g_codes, g_scales = g_mx[b]
+            f_codes, f_scales = f_mx[s]
+            out_rows = out[b].rearrange("(i t) n -> i t n", t=TILES)
+            n_cols = slice(half * HALF, (half + 1) * HALF)
+            y_ps = psum_y.tile([P, 2, HALF], F32, name="y_half_ps", tag="y_ps")
+            for k in range(2):
+                d_cols = slice((2 * pair + k) * P, (2 * pair + k + 1) * P)
+                nc.tensor.matmul_mx(
+                    out=y_ps[:, k, :],
+                    lhsT=g_codes[:, d_cols].bitcast(FP8X4),
+                    lhsT_scale=g_scales[:, d_cols],
+                    rhs=f_codes[:, n_cols].bitcast(FP8X4),
+                    rhs_scale=f_scales[:, n_cols],
+                    start=True,
+                    stop=True,
+                )
+            y_sb = results.tile([P, 2, HALF], F32, name="y_half_sb", tag="y_sb")
+            copy(out=y_sb[:], in_=y_ps[:])
+            first = c * CHUNK + half * HALF
+            nc.sync.dma_start(out=out_rows[:, 2 * pair : 2 * pair + 2, first : first + HALF], in_=y_sb[:])
+
         vector, scalar = nc.vector.tensor_copy, nc.scalar.copy
-        HALF = CHUNK // 2
 
         load_phi(0)
         load_theta(0, 0, 1)
@@ -222,18 +247,16 @@ def tile_nonlocalblocknd_pb_t_kernel(tc, theta_x, phi_x, g_x, out):
         quantise_theta(1, 0, CHUNK)
         new_theta(2)
         regroup_theta(vector, 2, 0, CHUNK)
-        quantise_f(0)
+        quantise_f(0, 0, CHUNK)
         quantise_g(0)
 
-        for s in range(STEPS):
+        for s in range(STEPS - 2):
             b, c = divmod(s, CHUNKS_PER_BATCH)
             prepare = b + 1 < BATCH
-            y_vector = (2, 3) if s + 2 == STEPS else (0, 2) if c == 3 or not prepare else (0,)
-            f_vector = (1, 3) if s + 2 == STEPS else ()
-            if s + 1 < STEPS:
-                new_f(s + 1)
-                for t in range(TILES):
-                    first_product(s + 1, t, t in f_vector)
+            y_vector = (0, 2) if c == 3 or not prepare else (0,)
+            new_f(s + 1)
+            for t in range(TILES):
+                first_product(s + 1, t)
             if s + 2 < STEPS:
                 quantise_theta(s + 2, 0, CHUNK)
             if prepare and c == 2:
@@ -243,12 +266,9 @@ def tile_nonlocalblocknd_pb_t_kernel(tc, theta_x, phi_x, g_x, out):
             if s + 3 < STEPS:
                 new_theta(s + 3)
                 regroup_theta(vector, s + 3, 0, CHUNK)
-            if s + 1 < STEPS and s + 2 == STEPS:
-                quantise_f(s + 1)
             for t in range(TILES):
                 second_product(vector if t in y_vector else scalar, s, t)
-            if s + 1 < STEPS and not (s + 2 == STEPS):
-                quantise_f(s + 1)
+            quantise_f(s + 1, 0, CHUNK)
             if prepare and c == 0:
                 new_phi(b + 1)
                 regroup_phi_rows(vector, b + 1, 0, P // 2)
@@ -256,3 +276,19 @@ def tile_nonlocalblocknd_pb_t_kernel(tc, theta_x, phi_x, g_x, out):
                 regroup_phi_rows(vector, b + 1, P // 2, P)
             if prepare and c == 2:
                 transpose_g(b + 1, (vector, scalar))
+
+        s = STEPS - 2
+        new_f(s + 1)
+        first_product(s + 1, 0)
+        first_product(s + 1, 1, True)
+        quantise_f(s + 1, 0, HALF)
+        second_product(scalar, s, 0)
+        second_product(scalar, s, 1)
+        first_product(s + 1, 3, True)
+        first_product(s + 1, 2)
+        second_product(vector, s, 3)
+        quantise_f(s + 1, HALF, CHUNK)
+        second_product(scalar, s, 2)
+        for half in range(2):
+            last_product(vector, half, 1)
+            last_product(scalar, half, 0)

@@ -129,6 +129,16 @@ def tile_nonlocalblocknd_pb_t_kernel(tc, theta_x, phi_x, g_x, out):
                 in_=theta_raw[s][:, :, n0:n1].rearrange("p j (c i) -> p c j i", i=8),
             )
 
+        def regroup_theta_gpsimd(s, n0, n1):
+            nc.gpsimd.tensor_scalar(
+                out=theta_grouped[s][:, n0:n1, :],
+                in0=theta_raw[s][:, :, n0:n1].rearrange("p j n -> p n j"),
+                scalar1=1.0,
+                scalar2=0.0,
+                op0=mybir.AluOpType.mult,
+                op1=mybir.AluOpType.add,
+            )
+
         def quantise_theta(s, n0, n1):
             quantise(theta_mx[s], theta_grouped[s][:].rearrange("p n j -> p (n j)"), n0, n1)
 
@@ -211,6 +221,7 @@ def tile_nonlocalblocknd_pb_t_kernel(tc, theta_x, phi_x, g_x, out):
             first = c * CHUNK + half * HALF
             nc.sync.dma_start(out=out_rows[:, 2 * pair : 2 * pair + 2, first : first + HALF], in_=y_sb[:])
 
+        SHARE = 416
         vector, scalar = nc.vector.tensor_copy, nc.scalar.copy
 
         load_phi(0)
@@ -265,7 +276,11 @@ def tile_nonlocalblocknd_pb_t_kernel(tc, theta_x, phi_x, g_x, out):
                 quantise_g(b + 1)
             if s + 3 < STEPS:
                 new_theta(s + 3)
-                regroup_theta(vector, s + 3, 0, CHUNK)
+                if len(y_vector) > 1:
+                    regroup_theta(vector, s + 3, 0, SHARE)
+                    regroup_theta_gpsimd(s + 3, SHARE - 8, CHUNK)
+                else:
+                    regroup_theta(vector, s + 3, 0, CHUNK)
             for t in range(TILES):
                 second_product(vector if t in y_vector else scalar, s, t)
             quantise_f(s + 1, 0, CHUNK)

@@ -264,7 +264,7 @@ def tile_nonlocalblocknd_pb_t_kernel(tc, theta_x, phi_x, g_x, out):
         for s in range(STEPS - 2):
             b, c = divmod(s, CHUNKS_PER_BATCH)
             prepare = b + 1 < BATCH
-            y_vector = (0, 2) if c == 3 or not prepare else (0,)
+            y_vector = (0, 2) if c == 3 or s == 5 or not prepare else (0,)
             new_f(s + 1)
             for t in range(TILES):
                 first_product(s + 1, t)
@@ -276,21 +276,21 @@ def tile_nonlocalblocknd_pb_t_kernel(tc, theta_x, phi_x, g_x, out):
                 quantise_g(b + 1)
             if s + 3 < STEPS:
                 new_theta(s + 3)
-                if len(y_vector) > 1:
+                if len(y_vector) > 1 or c == 2:
                     regroup_theta(vector, s + 3, 0, SHARE)
                     regroup_theta_gpsimd(s + 3, SHARE - 8, CHUNK)
                 else:
                     regroup_theta(vector, s + 3, 0, CHUNK)
             for t in range(TILES):
                 second_product(vector if t in y_vector else scalar, s, t)
+            if prepare and c == 2:
+                transpose_g(b + 1, (vector, scalar))
             quantise_f(s + 1, 0, CHUNK)
             if prepare and c == 0:
                 new_phi(b + 1)
                 regroup_phi_rows(vector, b + 1, 0, P // 2)
             if prepare and c == 1:
                 regroup_phi_rows(vector, b + 1, P // 2, P)
-            if prepare and c == 2:
-                transpose_g(b + 1, (vector, scalar))
 
         s = STEPS - 2
         new_f(s + 1)

from contextlib import ExitStack

import concourse.mybir as mybir
from concourse.masks import make_identity

BF16 = mybir.dt.bfloat16
F32 = mybir.dt.float32
U32 = mybir.dt.uint32
U8 = mybir.dt.uint8
FP8X4 = mybir.dt.float8_e4m3fn_x4

P = 128
PACK = 4
BATCH = 4
D = 512
N = 2048
NP = 512
CHUNK = 512
SUB = 128
CHUNKS_PER_BATCH = N // CHUNK
STEPS = BATCH * CHUNKS_PER_BATCH
TILES = 4

FLOPS = 2 * 2 * BATCH * N * NP * D


def tile_nonlocalblocknd_pb_t_kernel(tc, theta_x, phi_x, g_x, out):
    nc = tc.nc
    with ExitStack() as ctx:
        inputs = ctx.enter_context(tc.tile_pool(name="inputs", bufs=BATCH))
        consts = ctx.enter_context(tc.tile_pool(name="consts", bufs=1))
        weights = ctx.enter_context(tc.tile_pool(name="weights", bufs=2))
        stream = ctx.enter_context(tc.tile_pool(name="stream", bufs=3))
        results = ctx.enter_context(tc.tile_pool(name="results", bufs=8 * TILES))
        psum_f = ctx.enter_context(tc.psum_pool(name="psum_f", bufs=4))
        psum_y = ctx.enter_context(tc.psum_pool(name="psum_y", bufs=4))

        ctx.enter_context(tc.manual_schedule())

        HALF = CHUNK // 2
        theta_raw, phi_raw, g_raw = {}, {}, {}
        phi_grouped, g_grouped = {}, {}
        phi_mx, g_mx = {}, {}
        theta_grouped, theta_mx = {}, {}
        f_grouped, f_mx = {}, {}

        identity = consts.tile([P, P], F32, name="identity")
        make_identity(nc, identity[:])

        def load_phi(b):
            phi_raw[b] = inputs.tile([P, PACK, NP], BF16, name="phi_raw")
            nc.sync.dma_start(out=phi_raw[b][:], in_=phi_x[b].rearrange("(p j) m -> p j m", j=PACK))

        def load_g(b):
            g_raw[b] = inputs.tile([P, TILES * NP], BF16, name="g_raw")
            nc.sync.dma_start(out=g_raw[b][:], in_=g_x[b].rearrange("(i t) m -> i (t m)", t=TILES))

        def load_theta(b, chunk, chunks):
            rows = theta_x[b].rearrange("(p j) n -> p j n", j=PACK)
            raw = inputs.tile([P, PACK, chunks * CHUNK], BF16, name="theta_raw", tag="theta_raw%d" % chunks, bufs={1: 4, 2: 2, 4: 2}[chunks])
            nc.sync.dma_start(out=raw[:], in_=rows[:, :, chunk * CHUNK : (chunk + chunks) * CHUNK])
            for k in range(chunks):
                theta_raw[b * CHUNKS_PER_BATCH + chunk + k] = raw[:, :, k * CHUNK : (k + 1) * CHUNK]

        def new_phi(b):
            phi_grouped[b] = weights.tile(
                [P, TILES, P, PACK], BF16, name="phi_grouped", bufs=1, align_bytes=64
            )
            codes = weights.tile([P, NP], U32, name="phi_codes", align_bytes=64)
            scales = weights.tile([P, NP], U8, name="phi_scales", align_bytes=64)
            phi_mx[b] = codes, scales

        def regroup_phi_rows(copy, b, i0, i1):
            copy(
                out=phi_grouped[b][:, :, i0:i1].rearrange("p t i j -> p i j t"),
                in_=phi_raw[b][:, :, TILES * i0 : TILES * i1].rearrange("p j (i t) -> p i j t", t=TILES),
            )

        def regroup_phi(copy, b, t0, t1):
            copy(
                out=phi_grouped[b][:, t0:t1].rearrange("p t i j -> p i j t"),
                in_=phi_raw[b][:].rearrange("p j (i t) -> p i j t", t=TILES)[:, :, :, t0:t1],
            )

        def quantise_phi(b, t0, t1):
            quantise(phi_mx[b], phi_grouped[b][:].rearrange("p t i j -> p (t i j)"), t0 * P, t1 * P)

        def transpose_g(b, copies):
            g_words = g_raw[b][:].bitcast(F32).rearrange("i (t p u) -> i t u p", t=TILES, u=2)
            g_grouped[b] = weights.tile(
                [P, TILES * P * PACK], BF16, name="g_grouped", bufs=1, align_bytes=64
            )
            grouped_words = (
                g_grouped[b][:].bitcast(F32).rearrange("p (t i u) -> p t i u", t=TILES, u=2)
            )
            for pair in range(TILES // 2):
                g_ps = psum_f.tile([P, 2, 2, P], F32, name="g_ps", tag="f_ps")
                for t in range(2):
                    for u in range(2):
                        nc.tensor.transpose(
                            g_ps[:, t, u, :], g_words[:, 2 * pair + t, u, :], identity[:]
                        )
                copies[pair](
                    out=grouped_words[:, 2 * pair : 2 * pair + 2, :, :],
                    in_=g_ps[:].rearrange("p t u i -> p t i u"),
                )

        def quantise(operand, grouped, c0, c1):
            codes, scales = operand
            nc.vector.quantize_mx(
                out=codes[:, c0:c1].bitcast(FP8X4), scales=scales[:, c0:c1], in_=grouped[:, c0 * PACK : c1 * PACK]
            )

        def quantise_g(b):
            codes = weights.tile([P, D], U32, name="g_codes", align_bytes=64)
            scales = weights.tile([P, D], U8, name="g_scales", align_bytes=64)
            g_mx[b] = codes, scales
            quantise(g_mx[b], g_grouped[b][:], 0, D)

        def new_theta(s):
            theta_grouped[s] = stream.tile([P, CHUNK, PACK], BF16, name="theta_grouped", align_bytes=64)
            codes = stream.tile([P, CHUNK], U32, name="theta_codes", align_bytes=64)
            scales = stream.tile([P, CHUNK], U8, name="theta_scales", align_bytes=64)
            theta_mx[s] = codes, scales

        def regroup_theta(copy, s, n0, n1):
            copy(
                out=theta_grouped[s][:, n0:n1, :].rearrange("p (c i) j -> p c j i", i=8),
                in_=theta_raw[s][:, :, n0:n1].rearrange("p j (c i) -> p c j i", i=8),
            )

        def regroup_theta_gpsimd(s, n0, n1):
            nc.gpsimd.tensor_scalar(
                out=theta_grouped[s][:, n0:n1, :],
                in0=theta_raw[s][:, :, n0:n1].rearrange("p j n -> p n j"),
                scalar1=1.0,
                scalar2=0.0,
                op0=mybir.AluOpType.mult,
                op1=mybir.AluOpType.add,
            )

        def quantise_theta(s, n0, n1):
            quantise(theta_mx[s], theta_grouped[s][:].rearrange("p n j -> p (n j)"), n0, n1)

        def new_f(s):
            f_grouped[s] = stream.tile([P, CHUNK, PACK], BF16, name="f_grouped", align_bytes=64)

        def first_product(s, sub, on_vector=False):
            b = s // CHUNKS_PER_BATCH
            phi_codes, phi_scales = phi_mx[b]
            theta_codes, theta_scales = theta_mx[s]
            n_cols = slice(sub * SUB, (sub + 1) * SUB)
            f_ps = psum_f.tile([P, TILES, SUB], F32, name="f_ps")
            for t in range(TILES):
                m_cols = slice(t * P, (t + 1) * P)
                nc.tensor.matmul_mx(
                    out=f_ps[:, t, :],
                    lhsT=phi_codes[:, m_cols].bitcast(FP8X4),
                    lhsT_scale=phi_scales[:, m_cols],
                    rhs=theta_codes[:, n_cols].bitcast(FP8X4),
                    rhs_scale=theta_scales[:, n_cols],
                    start=True,
                    stop=True,
                )
            grouped, banked = f_grouped[s][:, n_cols, :], f_ps[:].rearrange("p t n -> p n t")
            if on_vector:
                nc.vector.tensor_scalar(
                    out=grouped, in0=banked, scalar1=1.0 / NP, scalar2=None, op0=mybir.AluOpType.mult
                )
            else:
                nc.scalar.mul(out=grouped, in_=banked, mul=1.0 / NP)

        def quantise_f(s, n0, n1):
            if n0 == 0:
                codes = stream.tile([P, CHUNK], U32, name="f_codes", align_bytes=64)
                scales = stream.tile([P, CHUNK], U8, name="f_scales", align_bytes=64)
                f_mx[s] = codes, scales
            quantise(f_mx[s], f_grouped[s][:].rearrange("p n t -> p (n t)"), n0, n1)

        def second_product(copy, s, t):
            b, c = divmod(s, CHUNKS_PER_BATCH)
            g_codes, g_scales = g_mx[b]
            f_codes, f_scales = f_mx[s]
            out_rows = out[b].rearrange("(i t) n -> i t n", t=TILES)
            d_cols = slice(t * P, (t + 1) * P)
            y_ps = psum_y.tile([P, CHUNK], F32, name="y_ps")
            nc.tensor.matmul_mx(
                out=y_ps[:],
                lhsT=g_codes[:, d_cols].bitcast(FP8X4),
                lhsT_scale=g_scales[:, d_cols],
                rhs=f_codes[:].bitcast(FP8X4),
                rhs_scale=f_scales[:],
                start=True,
                stop=True,
            )
            y_sb = results.tile([P, CHUNK], F32, name="y_sb")
            copy(out=y_sb[:], in_=y_ps[:])
            nc.sync.dma_start(out=out_rows[:, t, c * CHUNK : (c + 1) * CHUNK], in_=y_sb[:])

        def last_product(copy, half, pair):
            s = STEPS - 1
            b, c = divmod(s, CHUNKS_PER_BATCH)
            g_codes, g_scales = g_mx[b]
            f_codes, f_scales = f_mx[s]
            out_rows = out[b].rearrange("(i t) n -> i t n", t=TILES)
            n_cols = slice(half * HALF, (half + 1) * HALF)
            y_ps = psum_y.tile([P, 2, HALF], F32, name="y_half_ps", tag="y_ps")
            for k in range(2):
                d_cols = slice((2 * pair + k) * P, (2 * pair + k + 1) * P)
                nc.tensor.matmul_mx(
                    out=y_ps[:, k, :],
                    lhsT=g_codes[:, d_cols].bitcast(FP8X4),
                    lhsT_scale=g_scales[:, d_cols],
                    rhs=f_codes[:, n_cols].bitcast(FP8X4),
                    rhs_scale=f_scales[:, n_cols],
                    start=True,
                    stop=True,
                )
            y_sb = results.tile([P, 2, HALF], F32, name="y_half_sb", tag="y_sb")
            copy(out=y_sb[:], in_=y_ps[:])
            first = c * CHUNK + half * HALF
            nc.sync.dma_start(out=out_rows[:, 2 * pair : 2 * pair + 2, first : first + HALF], in_=y_sb[:])

        SHARE = 416
        vector, scalar = nc.vector.tensor_copy, nc.scalar.copy

        load_phi(0)
        load_theta(0, 0, 1)
        load_theta(0, 1, 1)
        load_g(0)
        load_theta(0, 2, 1)
        load_theta(0, 3, 1)
        load_theta(1, 0, 2)
        load_phi(1)
        load_theta(1, 2, 2)
        load_g(1)
        for b in range(2, BATCH):
            load_phi(b)
            load_theta(b, 0, 4)
            load_g(b)

        new_phi(0)
        new_theta(0)
        regroup_phi(vector, 0, 0, 2)
        regroup_phi(scalar, 0, 2, 4)
        quantise_phi(0, 0, 2)
        regroup_theta(vector, 0, 0, HALF)
        regroup_theta(scalar, 0, HALF, CHUNK)
        quantise_phi(0, 2, 4)
        quantise_theta(0, 0, HALF)
        quantise_theta(0, HALF, CHUNK)
        new_f(0)
        for sub in range(CHUNK // SUB):
            first_product(0, sub)
        new_theta(1)
        regroup_theta(vector, 1, 0, CHUNK)
        transpose_g(0, (scalar, scalar))
        quantise_theta(1, 0, CHUNK)
        new_theta(2)
        regroup_theta(vector, 2, 0, CHUNK)
        quantise_f(0, 0, CHUNK)
        quantise_g(0)

        for s in range(STEPS - 2):
            b, c = divmod(s, CHUNKS_PER_BATCH)
            prepare = b + 1 < BATCH
            y_vector = (0, 2) if c == 3 or s == 5 or not prepare else (0,)
            new_f(s + 1)
            for t in range(TILES):
                first_product(s + 1, t)
            if s + 2 < STEPS:
                quantise_theta(s + 2, 0, CHUNK)
            if prepare and c == 2:
                quantise_phi(b + 1, 0, TILES)
            if prepare and c == 3:
                quantise_g(b + 1)
            if s + 3 < STEPS:
                new_theta(s + 3)
                if len(y_vector) > 1 or c == 2:
                    regroup_theta(vector, s + 3, 0, SHARE)
                    regroup_theta_gpsimd(s + 3, SHARE - 8, CHUNK)
                else:
                    regroup_theta(vector, s + 3, 0, CHUNK)
            for t in range(TILES):
                second_product(vector if t in y_vector else scalar, s, t)
            if prepare and c == 2:
                transpose_g(b + 1, (vector, scalar))
            quantise_f(s + 1, 0, CHUNK)
            if prepare and c == 0:
                new_phi(b + 1)
                regroup_phi_rows(vector, b + 1, 0, P // 2)
            if prepare and c == 1:
                regroup_phi_rows(vector, b + 1, P // 2, P)

        s = STEPS - 2
        new_f(s + 1)
        first_product(s + 1, 0)
        first_product(s + 1, 1, True)
        quantise_f(s + 1, 0, HALF)
        second_product(scalar, s, 0)
        second_product(scalar, s, 1)
        first_product(s + 1, 3, True)
        first_product(s + 1, 2)
        second_product(vector, s, 3)
        quantise_f(s + 1, HALF, CHUNK)
        second_product(scalar, s, 2)
        for half in range(2):
            last_product(vector, half, 1)
            last_product(scalar, half, 0)
